import numpy as np
import ml_dtypes


def mxq(x, axis, fmt="e4m3"):
    dtype, down = {"e4m3": (ml_dtypes.float8_e4m3fn, 7), "e5m2": (ml_dtypes.float8_e5m2, 14)}[fmt]
    v = np.moveaxis(np.asarray(x, np.float32).astype(ml_dtypes.bfloat16).astype(np.float64), axis, -1)
    blocks = v.reshape(v.shape[:-1] + (-1, 32))
    amax = np.abs(blocks).max(-1, keepdims=True)
    byte = np.maximum(np.where(amax > 0, np.frexp(amax)[1] - 1 + 127, 0) - down, 1)
    scale = np.exp2(byte - 127.0)
    codes = (blocks / scale).astype(np.float32).astype(dtype).astype(np.float64)
    return np.moveaxis((codes * scale).reshape(v.shape), -1, axis)


WIDE = False


def mx_kscale(k):
    if not WIDE:
        return np.ones(k)
    levels = np.array([10, -10, 5, -5, 0])
    a = np.random.permutation(np.resize(levels, k // 512 * 4)).reshape(k // 512, 4)
    idx = np.arange(k)
    return np.exp2(a[idx // 512, idx % 128 // 32])


BF16 = ml_dtypes.bfloat16


def bf(x):
    return np.asarray(x, np.float32).astype(BF16)


def f64(x):
    return np.asarray(x).astype(np.float64)


B, SS, SM, SL, N, D = 1, 512, 1024, 1536, 512, 512
T = SS + SM + SL
EPS = 1e-5


def setup_inputs():
    s = mx_kscale(N)
    d = {"x": bf(np.random.standard_normal((B, T, N))),
         "gamma": bf((1.0 + 0.1 * np.random.standard_normal(N)) * s),
         "beta": bf(0.1 * np.random.standard_normal(N) * s)}
    for c in ("s", "m", "l"):
        d["Wqkv_" + c] = bf(np.random.standard_normal((N, 3 * D)) * 1.5 / np.sqrt(N) / s[:, None])
        d["bqkv_" + c] = bf(0.1 * np.random.standard_normal(3 * D))
    return d


def layer_norm(x, gamma, beta):
    mu = x.mean(-1, keepdims=True)
    var = np.square(x - mu).mean(-1, keepdims=True)
    return (x - mu) / np.sqrt(var + EPS) * gamma + beta


def proj(hseg, W, b):
    return (mxq(hseg, 2, "e4m3") @ mxq(f64(W), 0, "e4m3")) + f64(b)


def reference(x, gamma, beta, Wqkv_s, bqkv_s, Wqkv_m, bqkv_m, Wqkv_l, bqkv_l):
    h = layer_norm(f64(x), f64(gamma), f64(beta))
    qkv_s = proj(h[:, :SS], Wqkv_s, bqkv_s)
    qkv_m = proj(h[:, SS:SS + SM], Wqkv_m, bqkv_m)
    qkv_l = proj(h[:, SS + SM:T], Wqkv_l, bqkv_l)
    return np.concatenate([qkv_s, qkv_m, qkv_l], axis=1)

@@ -1,0 +1,202 @@
+from contextlib import ExitStack
+
+import concourse.mybir as mybir
+from concourse.masks import make_identity
+
+F32 = mybir.dt.float32
+BF16 = mybir.dt.bfloat16
+U32 = mybir.dt.uint32
+U8 = mybir.dt.uint8
+FP8X4 = mybir.dt.float8_e4m3fn_x4
+ACT = mybir.ActivationFunctionType
+ALU = mybir.AluOpType
+
+P = 128
+PACK = 4
+FEATURES = P * PACK
+OUT_COLS = 1536
+N_TILE = 512
+PIECES = OUT_COLS // N_TILE
+SEGMENT_TOKENS = (512, 1024, 1536)
+EPS = 1e-5
+GROUP = 2
+GROUP_TOKENS = GROUP * P
+CHUNKS_PER_BANK = N_TILE // GROUP_TOKENS
+
+FLOPS = 2 * sum(SEGMENT_TOKENS) * FEATURES * OUT_COLS
+
+
+def tile_multiscalesattn_pa_kernel(
+    tc, x, gamma, beta, Wqkv_s, bqkv_s, Wqkv_m, bqkv_m, Wqkv_l, bqkv_l, out
+):
+    nc = tc.nc
+    weights = (Wqkv_s, Wqkv_m, Wqkv_l)
+    biases = (bqkv_s, bqkv_m, bqkv_l)
+    n_scales = len(weights)
+
+    x_groups = x.flatten_outer_dims().rearrange("(g p i) k -> g p i k", p=P, i=GROUP)
+    out_groups = out.flatten_outer_dims().rearrange("(g p i) n -> g p i n", p=P, i=GROUP)
+    n_groups = sum(SEGMENT_TOKENS) // GROUP_TOKENS
+    first_group = [sum(SEGMENT_TOKENS[:c]) // GROUP_TOKENS for c in range(n_scales)]
+    scale_of_group = [max(c for c in range(n_scales) if first_group[c] <= g) for g in range(n_groups)]
+
+    with ExitStack() as ctx:
+        consts = ctx.enter_context(tc.tile_pool(name="consts", bufs=1))
+        small = ctx.enter_context(tc.tile_pool(name="small", bufs=6))
+        scratch = ctx.enter_context(tc.tile_pool(name="scratch", bufs=4))
+        work = ctx.enter_context(tc.tile_pool(name="work", bufs=3))
+        results = ctx.enter_context(tc.tile_pool(name="results", bufs=6))
+        psum_t = ctx.enter_context(tc.psum_pool(name="psum_t", bufs=4))
+        psum_acc = ctx.enter_context(tc.psum_pool(name="psum_acc", bufs=4))
+
+        x_all = consts.tile([P, n_groups, GROUP, FEATURES], BF16)
+        w_raw = [consts.tile([P, PACK, OUT_COLS], BF16, name="w_raw%d" % c) for c in range(n_scales)]
+        for c in range(n_scales):
+            last = first_group[c + 1] if c + 1 < n_scales else n_groups
+            for g in range(first_group[c], last):
+                nc.sync.dma_start(out=x_all[:, g, :, :], in_=x_groups[g])
+            nc.sync.dma_start(out=w_raw[c][:], in_=weights[c].rearrange("(j p) n -> p j n", p=P))
+
+        identity = consts.tile([P, P], F32)
+        make_identity(nc, identity[:])
+        eps = consts.tile([P, 1], F32)
+        nc.vector.memset(eps[:], EPS)
+
+        gb_rows = consts.tile([P, P], BF16)
+        nc.vector.memset(gb_rows[:], 0.0)
+        nc.scalar.dma_start(out=gb_rows[0:PACK, :], in_=gamma.rearrange("(j p) -> j p", p=P))
+        nc.scalar.dma_start(out=gb_rows[PACK : 2 * PACK, :], in_=beta.rearrange("(j p) -> j p", p=P))
+        gb_rows_f32 = consts.tile([P, P], F32)
+        nc.vector.tensor_copy(out=gb_rows_f32[:], in_=gb_rows[:])
+        gb_bank = psum_t.tile([P, P], F32, tag="xT")
+        nc.tensor.transpose(out=gb_bank[:], in_=gb_rows_f32[:], identity=identity[:])
+        gb_cols = consts.tile([P, 2 * PACK], F32)
+        nc.vector.tensor_copy(out=gb_cols[:], in_=gb_bank[:, 0 : 2 * PACK])
+
+        bias_rows = [consts.tile([P, OUT_COLS], BF16, name="bias_rows%d" % c) for c in range(n_scales)]
+        for c in range(n_scales):
+            nc.scalar.dma_start(out=bias_rows[c][:], in_=biases[c].partition_broadcast(P))
+
+        w_codes = [consts.tile([P, OUT_COLS], U32, name="w_codes%d" % c, align_bytes=64) for c in range(n_scales)]
+        w_scales = [consts.tile([P, OUT_COLS], U8, name="w_scales%d" % c, align_bytes=64) for c in range(n_scales)]
+
+        def prepare_weights(c, n):
+            cols = slice(n * N_TILE, (n + 1) * N_TILE)
+            w_grouped = work.tile([P, N_TILE, PACK], BF16, align_bytes=64)
+            src = w_raw[c][:, :, cols]
+            if c == 0:
+                nc.vector.tensor_copy(
+                    out=w_grouped[:].rearrange("p (c i) t -> p c t i", i=4),
+                    in_=src.rearrange("p t (c i) -> p c t i", i=4),
+                )
+            elif c == 1:
+                nc.scalar.copy(
+                    out=w_grouped[:].rearrange("p (c i) t -> p c t i", i=4),
+                    in_=src.rearrange("p t (c i) -> p c t i", i=4),
+                )
+            else:
+                nc.gpsimd.tensor_scalar(
+                    out=w_grouped[:], in0=src.rearrange("p t w -> p w t"),
+                    scalar1=1.0, scalar2=0.0, op0=ALU.mult, op1=ALU.add,
+                )
+            nc.vector.quantize_mx(
+                out=w_codes[c][:, cols].bitcast(FP8X4),
+                scales=w_scales[c][:, cols],
+                in_=w_grouped[:].rearrange("p w t -> p (w t)"),
+            )
+
+        neg_mean = {}
+        rstd = {}
+        xT = {}
+        h_codes = {}
+        h_scales = {}
+
+        def statistics(g):
+            neg_mean[g] = small.tile([P, GROUP], F32, name="neg_mean")
+            sum_sq = small.tile([P, GROUP], F32)
+            for i in range(GROUP):
+                unread = scratch.tile([P, FEATURES], BF16)
+                nc.scalar.activation(
+                    out=unread[:], in_=x_all[:, g, i, :], func=ACT.Copy, scale=-1.0 / FEATURES,
+                    accum_out=neg_mean[g][:, i : i + 1],
+                )
+            for i in range(GROUP):
+                unread = scratch.tile([P, FEATURES], BF16)
+                nc.scalar.activation(
+                    out=unread[:], in_=x_all[:, g, i, :], func=ACT.Square,
+                    bias=neg_mean[g][:, i : i + 1], scale=1.0, accum_out=sum_sq[:, i : i + 1],
+                )
+            std = small.tile([P, GROUP], F32)
+            nc.scalar.activation(out=std[:], in_=sum_sq[:], func=ACT.Sqrt, bias=eps[:, 0:1], scale=1.0 / FEATURES)
+            rstd[g] = small.tile([P, GROUP], F32, name="rstd")
+            nc.vector.reciprocal(out=rstd[g][:], in_=std[:])
+
+        def normalise_and_transpose(g):
+            xn = work.tile([P, GROUP, FEATURES], F32)
+            for i in range(GROUP):
+                nc.gpsimd.tensor_scalar(
+                    out=xn[:, i, :], in0=x_all[:, g, i, :],
+                    scalar1=neg_mean[g][:, i : i + 1], scalar2=rstd[g][:, i : i + 1],
+                    op0=ALU.add, op1=ALU.mult,
+                )
+            xT[g] = []
+            for b in range(PACK // CHUNKS_PER_BANK):
+                bank = psum_t.tile([P, CHUNKS_PER_BANK, GROUP_TOKENS], F32, name="xT", tag="xT")
+                xT[g].append(bank)
+                for jj in range(CHUNKS_PER_BANK):
+                    j = b * CHUNKS_PER_BANK + jj
+                    for i in range(GROUP):
+                        nc.tensor.transpose(
+                            out=bank[:, jj, i * P : (i + 1) * P],
+                            in_=xn[:, i, j * P : (j + 1) * P],
+                            identity=identity[:],
+                        )
+
+        def scale_shift_and_quantise(g):
+            hT = work.tile([P, PACK, GROUP_TOKENS], BF16)
+            for j in range(PACK):
+                nc.scalar.activation(
+                    out=hT[:, j, :], in_=xT[g][j // CHUNKS_PER_BANK][:, j % CHUNKS_PER_BANK, :],
+                    func=ACT.Identity, scale=gb_cols[:, j : j + 1], bias=gb_cols[:, PACK + j : PACK + j + 1],
+                )
+            h_grouped = work.tile([P, GROUP_TOKENS, PACK], BF16, align_bytes=64)
+            nc.gpsimd.tensor_scalar(
+                out=h_grouped[:], in0=hT[:].rearrange("p t w -> p w t"),
+                scalar1=1.0, scalar2=0.0, op0=ALU.mult, op1=ALU.add,
+            )
+            h_codes[g] = work.tile([P, GROUP_TOKENS], U32, name="h_codes", align_bytes=64)
+            h_scales[g] = work.tile([P, GROUP_TOKENS], U8, name="h_scales", align_bytes=64)
+            nc.vector.quantize_mx(
+                out=h_codes[g][:].bitcast(FP8X4), scales=h_scales[g][:],
+                in_=h_grouped[:].rearrange("p w t -> p (w t)"),
+            )
+
+        def project(g):
+            c = scale_of_group[g]
+            for i in range(GROUP):
+                tokens = slice(i * P, (i + 1) * P)
+                result = results.tile([P, OUT_COLS], F32)
+                for n in range(PIECES):
+                    cols = slice(n * N_TILE, (n + 1) * N_TILE)
+                    acc = psum_acc.tile([P, N_TILE], F32)
+                    nc.tensor.matmul_mx(
+                        out=acc[:],
+                        lhsT=h_codes[g][:, tokens].bitcast(FP8X4), lhsT_scale=h_scales[g][:, tokens],
+                        rhs=w_codes[c][:, cols].bitcast(FP8X4), rhs_scale=w_scales[c][:, cols],
+                        start=True, stop=True,
+                    )
+                    nc.vector.tensor_tensor(out=result[:, cols], in0=acc[:], in1=bias_rows[c][:, cols], op=ALU.add)
+                nc.sync.dma_start(out=out_groups[g, :, i, :], in_=result[:])
+
+        for step in range(n_groups + 3):
+            for c in range(n_scales):
+                if 0 <= step - first_group[c] < PIECES:
+                    prepare_weights(c, step - first_group[c])
+            if step < n_groups:
+                statistics(step)
+            if 0 <= step - 1 < n_groups:
+                normalise_and_transpose(step - 1)
+            if 0 <= step - 2 < n_groups:
+                scale_shift_and_quantise(step - 2)
+            if 0 <= step - 3 < n_groups:
+                project(step - 3)

@@ -73,9 +73,19 @@ def tile_multiscalesattn_pa_kernel(
         gb_cols = consts.tile([P, 2 * PACK], F32)
         nc.vector.tensor_copy(out=gb_cols[:], in_=gb_bank[:, 0 : 2 * PACK])
 
+        bias_src = consts.tile([P, n_scales, OUT_COLS], BF16)
+        nc.vector.memset(bias_src[:], 0.0)
+        ones = consts.tile([P, P], BF16)
+        nc.vector.memset(ones[:], 1.0)
         bias_rows = [consts.tile([P, OUT_COLS], BF16, name="bias_rows%d" % c) for c in range(n_scales)]
         for c in range(n_scales):
-            nc.scalar.dma_start(out=bias_rows[c][:], in_=biases[c].partition_broadcast(P))
+            nc.scalar.dma_start(out=bias_src[0:1, c, :], in_=biases[c].rearrange("(o n) -> o n", o=1))
+        for c in range(n_scales):
+            for n in range(PIECES):
+                cols = slice(n * N_TILE, (n + 1) * N_TILE)
+                bias_bank = psum_acc.tile([P, N_TILE], BF16, tag="acc")
+                nc.tensor.matmul(out=bias_bank[:], lhsT=ones[:], rhs=bias_src[:, c, cols], start=True, stop=True)
+                nc.vector.tensor_copy(out=bias_rows[c][:, cols], in_=bias_bank[:])
 
         w_codes = [consts.tile([P, OUT_COLS], U32, name="w_codes%d" % c, align_bytes=64) for c in range(n_scales)]
         w_scales = [consts.tile([P, OUT_COLS], U8, name="w_scales%d" % c, align_bytes=64) for c in range(n_scales)]

@@ -5,6 +5,7 @@ from concourse.masks import make_identity
 
 F32 = mybir.dt.float32
 BF16 = mybir.dt.bfloat16
+I32 = mybir.dt.int32
 U32 = mybir.dt.uint32
 U8 = mybir.dt.uint8
 FP8X4 = mybir.dt.float8_e4m3fn_x4
@@ -22,6 +23,7 @@ EPS = 1e-5
 GROUP = 2
 GROUP_TOKENS = GROUP * P
 CHUNKS_PER_BANK = N_TILE // GROUP_TOKENS
+RUN = 4
 
 FLOPS = 2 * sum(SEGMENT_TOKENS) * FEATURES * OUT_COLS
 
@@ -41,31 +43,42 @@ def tile_multiscalesattn_pa_kernel(
     scale_of_group = [max(c for c in range(n_scales) if first_group[c] <= g) for g in range(n_groups)]
 
     with ExitStack() as ctx:
+        ctx.enter_context(tc.manual_schedule())
         consts = ctx.enter_context(tc.tile_pool(name="consts", bufs=1))
-        small = ctx.enter_context(tc.tile_pool(name="small", bufs=6))
+        small = ctx.enter_context(tc.tile_pool(name="small", bufs=4))
         scratch = ctx.enter_context(tc.tile_pool(name="scratch", bufs=4))
         work = ctx.enter_context(tc.tile_pool(name="work", bufs=3))
         results = ctx.enter_context(tc.tile_pool(name="results", bufs=6))
         psum_t = ctx.enter_context(tc.psum_pool(name="psum_t", bufs=4))
         psum_acc = ctx.enter_context(tc.psum_pool(name="psum_acc", bufs=4))
 
+        gb_rows = consts.tile([P, P], BF16)
+        nc.vector.memset(gb_rows[:], 0.0)
+        nc.sync.dma_start(out=gb_rows[0:PACK, :], in_=gamma.rearrange("(j p) -> j p", p=P))
+        nc.sync.dma_start(out=gb_rows[PACK : 2 * PACK, :], in_=beta.rearrange("(j p) -> j p", p=P))
+        bias_src = consts.tile([P, n_scales * OUT_COLS], BF16)
+        nc.vector.memset(bias_src[:].bitcast(I32), 0)
+        for c in range(n_scales):
+            nc.scalar.dma_start(
+                out=bias_src[0:1, c * OUT_COLS : (c + 1) * OUT_COLS],
+                in_=biases[c].rearrange("(o n) -> o n", o=1),
+            )
+
         x_all = consts.tile([P, n_groups, GROUP, FEATURES], BF16)
         w_raw = [consts.tile([P, PACK, OUT_COLS], BF16, name="w_raw%d" % c) for c in range(n_scales)]
-        for c in range(n_scales):
-            last = first_group[c + 1] if c + 1 < n_scales else n_groups
-            for g in range(first_group[c], last):
-                nc.sync.dma_start(out=x_all[:, g, :, :], in_=x_groups[g])
-            nc.sync.dma_start(out=w_raw[c][:], in_=weights[c].rearrange("(j p) n -> p j n", p=P))
+        for g in range(n_groups):
+            nc.sync.dma_start(out=x_all[:, g, :, :], in_=x_groups[g])
+            c = scale_of_group[g]
+            if g == first_group[c] + 1:
+                nc.sync.dma_start(out=w_raw[c][:], in_=weights[c].rearrange("(j p) n -> p j n", p=P))
 
         identity = consts.tile([P, P], F32)
         make_identity(nc, identity[:])
         eps = consts.tile([P, 1], F32)
         nc.vector.memset(eps[:], EPS)
+        ones = consts.tile([P, P], BF16)
+        nc.vector.memset(ones[:], 1.0)
 
-        gb_rows = consts.tile([P, P], BF16)
-        nc.vector.memset(gb_rows[:], 0.0)
-        nc.scalar.dma_start(out=gb_rows[0:PACK, :], in_=gamma.rearrange("(j p) -> j p", p=P))
-        nc.scalar.dma_start(out=gb_rows[PACK : 2 * PACK, :], in_=beta.rearrange("(j p) -> j p", p=P))
         gb_rows_f32 = consts.tile([P, P], F32)
         nc.vector.tensor_copy(out=gb_rows_f32[:], in_=gb_rows[:])
         gb_bank = psum_t.tile([P, P], F32, tag="xT")
@@ -73,51 +86,50 @@ def tile_multiscalesattn_pa_kernel(
         gb_cols = consts.tile([P, 2 * PACK], F32)
         nc.vector.tensor_copy(out=gb_cols[:], in_=gb_bank[:, 0 : 2 * PACK])
 
-        bias_src = consts.tile([P, n_scales, OUT_COLS], BF16)
-        nc.vector.memset(bias_src[:], 0.0)
-        ones = consts.tile([P, P], BF16)
-        nc.vector.memset(ones[:], 1.0)
-        bias_rows = [consts.tile([P, OUT_COLS], BF16, name="bias_rows%d" % c) for c in range(n_scales)]
-        for c in range(n_scales):
-            nc.scalar.dma_start(out=bias_src[0:1, c, :], in_=biases[c].rearrange("(o n) -> o n", o=1))
-        for c in range(n_scales):
-            for n in range(PIECES):
-                cols = slice(n * N_TILE, (n + 1) * N_TILE)
-                bias_bank = psum_acc.tile([P, N_TILE], BF16, tag="acc")
-                nc.tensor.matmul(out=bias_bank[:], lhsT=ones[:], rhs=bias_src[:, c, cols], start=True, stop=True)
-                nc.vector.tensor_copy(out=bias_rows[c][:, cols], in_=bias_bank[:])
+        bias_rows = consts.tile([P, n_scales * OUT_COLS], BF16)
+
+        def spread_bias(piece):
+            cols = slice(piece * N_TILE, (piece + 1) * N_TILE)
+            bias_bank = psum_acc.tile([P, N_TILE], BF16, tag="acc")
+            nc.tensor.matmul(out=bias_bank[:], lhsT=ones[:], rhs=bias_src[:, cols], start=True, stop=True)
+            nc.vector.tensor_copy(out=bias_rows[:, cols], in_=bias_bank[:])
 
         w_codes = [consts.tile([P, OUT_COLS], U32, name="w_codes%d" % c, align_bytes=64) for c in range(n_scales)]
         w_scales = [consts.tile([P, OUT_COLS], U8, name="w_scales%d" % c, align_bytes=64) for c in range(n_scales)]
+        w_grouped = {}
 
-        def prepare_weights(c, n):
-            cols = slice(n * N_TILE, (n + 1) * N_TILE)
-            w_grouped = work.tile([P, N_TILE, PACK], BF16, align_bytes=64)
-            src = w_raw[c][:, :, cols]
-            if c == 0:
-                nc.vector.tensor_copy(
-                    out=w_grouped[:].rearrange("p (c i) t -> p c t i", i=4),
-                    in_=src.rearrange("p t (c i) -> p c t i", i=4),
-                )
-            elif c == 1:
-                nc.scalar.copy(
-                    out=w_grouped[:].rearrange("p (c i) t -> p c t i", i=4),
-                    in_=src.rearrange("p t (c i) -> p c t i", i=4),
+        def regroup_weights(piece, engine):
+            c, n = divmod(piece, PIECES)
+            w_grouped[piece] = work.tile([P, N_TILE, PACK], BF16, name="w_grouped", align_bytes=64)
+            dst = w_grouped[piece][:]
+            src = w_raw[c][:, :, n * N_TILE : (n + 1) * N_TILE]
+            if engine == "gpsimd":
+                nc.gpsimd.tensor_scalar(
+                    out=dst, in0=src.rearrange("p j w -> p w j"), scalar1=1.0, scalar2=0.0, op0=ALU.mult, op1=ALU.add
                 )
             else:
-                nc.gpsimd.tensor_scalar(
-                    out=w_grouped[:], in0=src.rearrange("p t w -> p w t"),
-                    scalar1=1.0, scalar2=0.0, op0=ALU.mult, op1=ALU.add,
-                )
+                dst_runs = dst.rearrange("p (w r) j -> p w j r", r=RUN)
+                src_runs = src.rearrange("p j (w r) -> p w j r", r=RUN)
+                if engine == "vector":
+                    nc.vector.tensor_copy(out=dst_runs, in_=src_runs)
+                else:
+                    nc.scalar.copy(out=dst_runs, in_=src_runs)
+
+        def quantise_weights(piece):
+            c, n = divmod(piece, PIECES)
+            cols = slice(n * N_TILE, (n + 1) * N_TILE)
             nc.vector.quantize_mx(
                 out=w_codes[c][:, cols].bitcast(FP8X4),
                 scales=w_scales[c][:, cols],
-                in_=w_grouped[:].rearrange("p w t -> p (w t)"),
+                in_=w_grouped[piece][:].rearrange("p w j -> p (w j)"),
             )
 
         neg_mean = {}
+        std = {}
         rstd = {}
         xT = {}
+        hT = {}
+        h_grouped = {}
         h_codes = {}
         h_scales = {}
 
@@ -136,10 +148,12 @@ def tile_multiscalesattn_pa_kernel(
                     out=unread[:], in_=x_all[:, g, i, :], func=ACT.Square,
                     bias=neg_mean[g][:, i : i + 1], scale=1.0, accum_out=sum_sq[:, i : i + 1],
                 )
-            std = small.tile([P, GROUP], F32)
-            nc.scalar.activation(out=std[:], in_=sum_sq[:], func=ACT.Sqrt, bias=eps[:, 0:1], scale=1.0 / FEATURES)
+            std[g] = small.tile([P, GROUP], F32, name="std")
+            nc.scalar.activation(out=std[g][:], in_=sum_sq[:], func=ACT.Sqrt, bias=eps[:, 0:1], scale=1.0 / FEATURES)
+
+        def reciprocal(g):
             rstd[g] = small.tile([P, GROUP], F32, name="rstd")
-            nc.vector.reciprocal(out=rstd[g][:], in_=std[:])
+            nc.vector.reciprocal(out=rstd[g][:], in_=std[g][:])
 
         def normalise_and_transpose(g):
             xn = work.tile([P, GROUP, FEATURES], F32)
@@ -162,51 +176,78 @@ def tile_multiscalesattn_pa_kernel(
                             identity=identity[:],
                         )
 
-        def scale_shift_and_quantise(g):
-            hT = work.tile([P, PACK, GROUP_TOKENS], BF16)
+        def scale_and_shift(g):
+            hT[g] = work.tile([P, PACK, GROUP_TOKENS], BF16, name="hT")
             for j in range(PACK):
                 nc.scalar.activation(
-                    out=hT[:, j, :], in_=xT[g][j // CHUNKS_PER_BANK][:, j % CHUNKS_PER_BANK, :],
+                    out=hT[g][:, j, :], in_=xT[g][j // CHUNKS_PER_BANK][:, j % CHUNKS_PER_BANK, :],
                     func=ACT.Identity, scale=gb_cols[:, j : j + 1], bias=gb_cols[:, PACK + j : PACK + j + 1],
                 )
-            h_grouped = work.tile([P, GROUP_TOKENS, PACK], BF16, align_bytes=64)
+
+        def regroup(g):
+            h_grouped[g] = work.tile([P, GROUP_TOKENS, PACK], BF16, name="h_grouped", align_bytes=64)
             nc.gpsimd.tensor_scalar(
-                out=h_grouped[:], in0=hT[:].rearrange("p t w -> p w t"),
+                out=h_grouped[g][:], in0=hT[g][:].rearrange("p j w -> p w j"),
                 scalar1=1.0, scalar2=0.0, op0=ALU.mult, op1=ALU.add,
             )
+
+        def quantise(g):
             h_codes[g] = work.tile([P, GROUP_TOKENS], U32, name="h_codes", align_bytes=64)
             h_scales[g] = work.tile([P, GROUP_TOKENS], U8, name="h_scales", align_bytes=64)
             nc.vector.quantize_mx(
                 out=h_codes[g][:].bitcast(FP8X4), scales=h_scales[g][:],
-                in_=h_grouped[:].rearrange("p w t -> p (w t)"),
+                in_=h_grouped[g][:].rearrange("p w j -> p (w j)"),
             )
 
-        def project(g):
+        def project(g, i):
             c = scale_of_group[g]
-            for i in range(GROUP):
-                tokens = slice(i * P, (i + 1) * P)
-                result = results.tile([P, OUT_COLS], F32)
-                for n in range(PIECES):
-                    cols = slice(n * N_TILE, (n + 1) * N_TILE)
-                    acc = psum_acc.tile([P, N_TILE], F32)
-                    nc.tensor.matmul_mx(
-                        out=acc[:],
-                        lhsT=h_codes[g][:, tokens].bitcast(FP8X4), lhsT_scale=h_scales[g][:, tokens],
-                        rhs=w_codes[c][:, cols].bitcast(FP8X4), rhs_scale=w_scales[c][:, cols],
-                        start=True, stop=True,
-                    )
-                    nc.vector.tensor_tensor(out=result[:, cols], in0=acc[:], in1=bias_rows[c][:, cols], op=ALU.add)
-                nc.sync.dma_start(out=out_groups[g, :, i, :], in_=result[:])
+            tokens = slice(i * P, (i + 1) * P)
+            result = results.tile([P, OUT_COLS], F32)
+            for n in range(PIECES):
+                cols = slice(n * N_TILE, (n + 1) * N_TILE)
+                acc = psum_acc.tile([P, N_TILE], F32, tag="acc")
+                nc.tensor.matmul_mx(
+                    out=acc[:],
+                    lhsT=h_codes[g][:, tokens].bitcast(FP8X4), lhsT_scale=h_scales[g][:, tokens],
+                    rhs=w_codes[c][:, cols].bitcast(FP8X4), rhs_scale=w_scales[c][:, cols],
+                    start=True, stop=True,
+                )
+                nc.vector.tensor_tensor(
+                    out=result[:, cols], in0=acc[:],
+                    in1=bias_rows[:, c * OUT_COLS + n * N_TILE : c * OUT_COLS + (n + 1) * N_TILE], op=ALU.add,
+                )
+            nc.sync.dma_start(out=out_groups[g, :, i, :], in_=result[:])
 
-        for step in range(n_groups + 3):
-            for c in range(n_scales):
-                if 0 <= step - first_group[c] < PIECES:
-                    prepare_weights(c, step - first_group[c])
-            if step < n_groups:
+        n_pieces = n_scales * PIECES
+        regroup_step = [1 if piece < PIECES else 2 + (piece - PIECES) // 2 for piece in range(n_pieces)]
+
+        def in_range(g):
+            return 0 <= g < n_groups
+
+        for step in range(n_groups + 4):
+            if in_range(step - 1):
+                reciprocal(step - 1)
+            if in_range(step - 3):
+                quantise(step - 3)
+            if in_range(step - 4):
+                project(step - 4, 1)
+            if in_range(step - 3):
+                project(step - 3, 0)
+            for piece in range(n_pieces):
+                if regroup_step[piece] == step - 1:
+                    quantise_weights(piece)
+                    spread_bias(piece)
+            if in_range(step - 2):
+                scale_and_shift(step - 2)
+            if in_range(step):
                 statistics(step)
-            if 0 <= step - 1 < n_groups:
+            if in_range(step - 1):
                 normalise_and_transpose(step - 1)
-            if 0 <= step - 2 < n_groups:
-                scale_shift_and_quantise(step - 2)
-            if 0 <= step - 3 < n_groups:
-                project(step - 3)
+            if in_range(step - 2):
+                regroup(step - 2)
+            for piece in range(n_pieces):
+                if regroup_step[piece] == step:
+                    if piece < PIECES:
+                        regroup_weights(piece, "vector")
+                    else:
+                        regroup_weights(piece, "scalar" if piece % 2 == 1 else "gpsimd")

@@ -48,7 +48,7 @@ def tile_multiscalesattn_pa_kernel(
         small = ctx.enter_context(tc.tile_pool(name="small", bufs=4))
         scratch = ctx.enter_context(tc.tile_pool(name="scratch", bufs=4))
         work = ctx.enter_context(tc.tile_pool(name="work", bufs=3))
-        results = ctx.enter_context(tc.tile_pool(name="results", bufs=6))
+        results = ctx.enter_context(tc.tile_pool(name="results", bufs=12))
         psum_t = ctx.enter_context(tc.psum_pool(name="psum_t", bufs=4))
         psum_acc = ctx.enter_context(tc.psum_pool(name="psum_acc", bufs=4))
 
@@ -132,6 +132,7 @@ def tile_multiscalesattn_pa_kernel(
         h_grouped = {}
         h_codes = {}
         h_scales = {}
+        unbiased = {}
 
         def statistics(g):
             neg_mean[g] = small.tile([P, GROUP], F32, name="neg_mean")
@@ -199,10 +200,12 @@ def tile_multiscalesattn_pa_kernel(
                 in_=h_grouped[g][:].rearrange("p w j -> p (w j)"),
             )
 
+        def goes_round_vector(g, i, n):
+            return scale_of_group[g] == n_scales - 1 and i == GROUP - 1 and n == PIECES - 1
+
         def project(g, i):
             c = scale_of_group[g]
             tokens = slice(i * P, (i + 1) * P)
-            result = results.tile([P, OUT_COLS], F32)
             for n in range(PIECES):
                 cols = slice(n * N_TILE, (n + 1) * N_TILE)
                 acc = psum_acc.tile([P, N_TILE], F32, tag="acc")
@@ -212,11 +215,25 @@ def tile_multiscalesattn_pa_kernel(
                     rhs=w_codes[c][:, cols].bitcast(FP8X4), rhs_scale=w_scales[c][:, cols],
                     start=True, stop=True,
                 )
-                nc.vector.tensor_tensor(
-                    out=result[:, cols], in0=acc[:],
-                    in1=bias_rows[:, c * OUT_COLS + n * N_TILE : c * OUT_COLS + (n + 1) * N_TILE], op=ALU.add,
+                if goes_round_vector(g, i, n):
+                    unbiased[g] = work.tile([P, N_TILE], F32, name="unbiased")
+                    nc.scalar.copy(out=unbiased[g][:], in_=acc[:])
+                else:
+                    result = results.tile([P, N_TILE], F32)
+                    nc.vector.tensor_tensor(
+                        out=result[:], in0=acc[:], in1=bias_rows[:, c * OUT_COLS + n * N_TILE :][:, :N_TILE], op=ALU.add
+                    )
+                    nc.sync.dma_start(out=out_groups[g, :, i, cols], in_=result[:])
+
+        def finish_on_gpsimd(g):
+            i, n = GROUP - 1, PIECES - 1
+            if goes_round_vector(g, i, n):
+                c = scale_of_group[g]
+                result = results.tile([P, N_TILE], F32)
+                nc.gpsimd.tensor_tensor(
+                    out=result[:], in0=unbiased[g][:], in1=bias_rows[:, c * OUT_COLS + n * N_TILE :][:, :N_TILE], op=ALU.add
                 )
-            nc.sync.dma_start(out=out_groups[g, :, i, :], in_=result[:])
+                nc.sync.dma_start(out=out_groups[g, :, i, n * N_TILE : (n + 1) * N_TILE], in_=result[:])
 
         n_pieces = n_scales * PIECES
         regroup_step = [1 if piece < PIECES else 2 + (piece - PIECES) // 2 for piece in range(n_pieces)]
@@ -245,6 +262,8 @@ def tile_multiscalesattn_pa_kernel(
                 normalise_and_transpose(step - 1)
             if in_range(step - 2):
                 regroup(step - 2)
+            if in_range(step - 4):
+                finish_on_gpsimd(step - 4)
             for piece in range(n_pieces):
                 if regroup_step[piece] == step:
                     if piece < PIECES:

from contextlib import ExitStack

import concourse.mybir as mybir
from concourse.masks import make_identity

F32 = mybir.dt.float32
BF16 = mybir.dt.bfloat16
I32 = mybir.dt.int32
U32 = mybir.dt.uint32
U8 = mybir.dt.uint8
FP8X4 = mybir.dt.float8_e4m3fn_x4
ACT = mybir.ActivationFunctionType
ALU = mybir.AluOpType

P = 128
PACK = 4
FEATURES = P * PACK
OUT_COLS = 1536
N_TILE = 512
PIECES = OUT_COLS // N_TILE
SEGMENT_TOKENS = (512, 1024, 1536)
EPS = 1e-5
GROUP = 2
GROUP_TOKENS = GROUP * P
CHUNKS_PER_BANK = N_TILE // GROUP_TOKENS
RUN = 4

FLOPS = 2 * sum(SEGMENT_TOKENS) * FEATURES * OUT_COLS


def tile_multiscalesattn_pa_kernel(
    tc, x, gamma, beta, Wqkv_s, bqkv_s, Wqkv_m, bqkv_m, Wqkv_l, bqkv_l, out
):
    nc = tc.nc
    weights = (Wqkv_s, Wqkv_m, Wqkv_l)
    biases = (bqkv_s, bqkv_m, bqkv_l)
    n_scales = len(weights)

    x_groups = x.flatten_outer_dims().rearrange("(g p i) k -> g p i k", p=P, i=GROUP)
    out_groups = out.flatten_outer_dims().rearrange("(g p i) n -> g p i n", p=P, i=GROUP)
    n_groups = sum(SEGMENT_TOKENS) // GROUP_TOKENS
    first_group = [sum(SEGMENT_TOKENS[:c]) // GROUP_TOKENS for c in range(n_scales)]
    scale_of_group = [max(c for c in range(n_scales) if first_group[c] <= g) for g in range(n_groups)]

    with ExitStack() as ctx:
        ctx.enter_context(tc.manual_schedule())
        consts = ctx.enter_context(tc.tile_pool(name="consts", bufs=1))
        small = ctx.enter_context(tc.tile_pool(name="small", bufs=4))
        scratch = ctx.enter_context(tc.tile_pool(name="scratch", bufs=4))
        work = ctx.enter_context(tc.tile_pool(name="work", bufs=3))
        results = ctx.enter_context(tc.tile_pool(name="results", bufs=12))
        psum_t = ctx.enter_context(tc.psum_pool(name="psum_t", bufs=4))
        psum_acc = ctx.enter_context(tc.psum_pool(name="psum_acc", bufs=4))

        gb_rows = consts.tile([P, P], BF16)
        nc.vector.memset(gb_rows[:], 0.0)
        nc.sync.dma_start(out=gb_rows[0:PACK, :], in_=gamma.rearrange("(j p) -> j p", p=P))
        nc.sync.dma_start(out=gb_rows[PACK : 2 * PACK, :], in_=beta.rearrange("(j p) -> j p", p=P))
        bias_src = consts.tile([P, n_scales * OUT_COLS], BF16)
        nc.vector.memset(bias_src[:].bitcast(I32), 0)
        for c in range(n_scales):
            nc.scalar.dma_start(
                out=bias_src[0:1, c * OUT_COLS : (c + 1) * OUT_COLS],
                in_=biases[c].rearrange("(o n) -> o n", o=1),
            )

        x_all = consts.tile([P, n_groups, GROUP, FEATURES], BF16)
        w_raw = [consts.tile([P, PACK, OUT_COLS], BF16, name="w_raw%d" % c) for c in range(n_scales)]
        for g in range(n_groups):
            nc.sync.dma_start(out=x_all[:, g, :, :], in_=x_groups[g])
            c = scale_of_group[g]
            if g == first_group[c] + 1:
                nc.sync.dma_start(out=w_raw[c][:], in_=weights[c].rearrange("(j p) n -> p j n", p=P))

        identity = consts.tile([P, P], F32)
        make_identity(nc, identity[:])
        eps = consts.tile([P, 1], F32)
        nc.vector.memset(eps[:], EPS)
        ones = consts.tile([P, P], BF16)
        nc.vector.memset(ones[:], 1.0)

        gb_rows_f32 = consts.tile([P, P], F32)
        nc.vector.tensor_copy(out=gb_rows_f32[:], in_=gb_rows[:])
        gb_bank = psum_t.tile([P, P], F32, tag="xT")
        nc.tensor.transpose(out=gb_bank[:], in_=gb_rows_f32[:], identity=identity[:])
        gb_cols = consts.tile([P, 2 * PACK], F32)
        nc.vector.tensor_copy(out=gb_cols[:], in_=gb_bank[:, 0 : 2 * PACK])

        bias_rows = consts.tile([P, n_scales * OUT_COLS], BF16)

        def spread_bias(piece):
            cols = slice(piece * N_TILE, (piece + 1) * N_TILE)
            bias_bank = psum_acc.tile([P, N_TILE], BF16, tag="acc")
            nc.tensor.matmul(out=bias_bank[:], lhsT=ones[:], rhs=bias_src[:, cols], start=True, stop=True)
            nc.vector.tensor_copy(out=bias_rows[:, cols], in_=bias_bank[:])

        w_codes = [consts.tile([P, OUT_COLS], U32, name="w_codes%d" % c, align_bytes=64) for c in range(n_scales)]
        w_scales = [consts.tile([P, OUT_COLS], U8, name="w_scales%d" % c, align_bytes=64) for c in range(n_scales)]
        w_grouped = {}

        def regroup_weights(piece, engine):
            c, n = divmod(piece, PIECES)
            w_grouped[piece] = work.tile([P, N_TILE, PACK], BF16, name="w_grouped", align_bytes=64)
            dst = w_grouped[piece][:]
            src = w_raw[c][:, :, n * N_TILE : (n + 1) * N_TILE]
            if engine == "gpsimd":
                nc.gpsimd.tensor_scalar(
                    out=dst, in0=src.rearrange("p j w -> p w j"), scalar1=1.0, scalar2=0.0, op0=ALU.mult, op1=ALU.add
                )
            else:
                dst_runs = dst.rearrange("p (w r) j -> p w j r", r=RUN)
                src_runs = src.rearrange("p j (w r) -> p w j r", r=RUN)
                if engine == "vector":
                    nc.vector.tensor_copy(out=dst_runs, in_=src_runs)
                else:
                    nc.scalar.copy(out=dst_runs, in_=src_runs)

        def quantise_weights(piece):
            c, n = divmod(piece, PIECES)
            cols = slice(n * N_TILE, (n + 1) * N_TILE)
            nc.vector.quantize_mx(
                out=w_codes[c][:, cols].bitcast(FP8X4),
                scales=w_scales[c][:, cols],
                in_=w_grouped[piece][:].rearrange("p w j -> p (w j)"),
            )

        neg_mean = {}
        std = {}
        rstd = {}
        xT = {}
        hT = {}
        h_grouped = {}
        h_codes = {}
        h_scales = {}
        unbiased = {}

        def statistics(g):
            neg_mean[g] = small.tile([P, GROUP], F32, name="neg_mean")
            sum_sq = small.tile([P, GROUP], F32)
            for i in range(GROUP):
                unread = scratch.tile([P, FEATURES], BF16)
                nc.scalar.activation(
                    out=unread[:], in_=x_all[:, g, i, :], func=ACT.Copy, scale=-1.0 / FEATURES,
                    accum_out=neg_mean[g][:, i : i + 1],
                )
            for i in range(GROUP):
                unread = scratch.tile([P, FEATURES], BF16)
                nc.scalar.activation(
                    out=unread[:], in_=x_all[:, g, i, :], func=ACT.Square,
                    bias=neg_mean[g][:, i : i + 1], scale=1.0, accum_out=sum_sq[:, i : i + 1],
                )
            std[g] = small.tile([P, GROUP], F32, name="std")
            nc.scalar.activation(out=std[g][:], in_=sum_sq[:], func=ACT.Sqrt, bias=eps[:, 0:1], scale=1.0 / FEATURES)

        def reciprocal(g):
            rstd[g] = small.tile([P, GROUP], F32, name="rstd")
            nc.vector.reciprocal(out=rstd[g][:], in_=std[g][:])

        def normalise_and_transpose(g):
            xn = work.tile([P, GROUP, FEATURES], F32)
            for i in range(GROUP):
                nc.gpsimd.tensor_scalar(
                    out=xn[:, i, :], in0=x_all[:, g, i, :],
                    scalar1=neg_mean[g][:, i : i + 1], scalar2=rstd[g][:, i : i + 1],
                    op0=ALU.add, op1=ALU.mult,
                )
            xT[g] = []
            for b in range(PACK // CHUNKS_PER_BANK):
                bank = psum_t.tile([P, CHUNKS_PER_BANK, GROUP_TOKENS], F32, name="xT", tag="xT")
                xT[g].append(bank)
                for jj in range(CHUNKS_PER_BANK):
                    j = b * CHUNKS_PER_BANK + jj
                    for i in range(GROUP):
                        nc.tensor.transpose(
                            out=bank[:, jj, i * P : (i + 1) * P],
                            in_=xn[:, i, j * P : (j + 1) * P],
                            identity=identity[:],
                        )

        def scale_and_shift(g):
            hT[g] = work.tile([P, PACK, GROUP_TOKENS], BF16, name="hT")
            for j in range(PACK):
                nc.scalar.activation(
                    out=hT[g][:, j, :], in_=xT[g][j // CHUNKS_PER_BANK][:, j % CHUNKS_PER_BANK, :],
                    func=ACT.Identity, scale=gb_cols[:, j : j + 1], bias=gb_cols[:, PACK + j : PACK + j + 1],
                )

        def regroup(g):
            h_grouped[g] = work.tile([P, GROUP_TOKENS, PACK], BF16, name="h_grouped", align_bytes=64)
            nc.gpsimd.tensor_scalar(
                out=h_grouped[g][:], in0=hT[g][:].rearrange("p j w -> p w j"),
                scalar1=1.0, scalar2=0.0, op0=ALU.mult, op1=ALU.add,
            )

        def quantise(g):
            h_codes[g] = work.tile([P, GROUP_TOKENS], U32, name="h_codes", align_bytes=64)
            h_scales[g] = work.tile([P, GROUP_TOKENS], U8, name="h_scales", align_bytes=64)
            nc.vector.quantize_mx(
                out=h_codes[g][:].bitcast(FP8X4), scales=h_scales[g][:],
                in_=h_grouped[g][:].rearrange("p w j -> p (w j)"),
            )

        def goes_round_vector(g, i, n):
            return scale_of_group[g] == n_scales - 1 and i == GROUP - 1 and n == PIECES - 1

        def project(g, i):
            c = scale_of_group[g]
            tokens = slice(i * P, (i + 1) * P)
            for n in range(PIECES):
                cols = slice(n * N_TILE, (n + 1) * N_TILE)
                acc = psum_acc.tile([P, N_TILE], F32, tag="acc")
                nc.tensor.matmul_mx(
                    out=acc[:],
                    lhsT=h_codes[g][:, tokens].bitcast(FP8X4), lhsT_scale=h_scales[g][:, tokens],
                    rhs=w_codes[c][:, cols].bitcast(FP8X4), rhs_scale=w_scales[c][:, cols],
                    start=True, stop=True,
                )
                if goes_round_vector(g, i, n):
                    unbiased[g] = work.tile([P, N_TILE], F32, name="unbiased")
                    nc.scalar.copy(out=unbiased[g][:], in_=acc[:])
                else:
                    result = results.tile([P, N_TILE], F32)
                    nc.vector.tensor_tensor(
                        out=result[:], in0=acc[:], in1=bias_rows[:, c * OUT_COLS + n * N_TILE :][:, :N_TILE], op=ALU.add
                    )
                    nc.sync.dma_start(out=out_groups[g, :, i, cols], in_=result[:])

        def finish_on_gpsimd(g):
            i, n = GROUP - 1, PIECES - 1
            if goes_round_vector(g, i, n):
                c = scale_of_group[g]
                result = results.tile([P, N_TILE], F32)
                nc.gpsimd.tensor_tensor(
                    out=result[:], in0=unbiased[g][:], in1=bias_rows[:, c * OUT_COLS + n * N_TILE :][:, :N_TILE], op=ALU.add
                )
                nc.sync.dma_start(out=out_groups[g, :, i, n * N_TILE : (n + 1) * N_TILE], in_=result[:])

        n_pieces = n_scales * PIECES
        regroup_step = [1 if piece < PIECES else 2 + (piece - PIECES) // 2 for piece in range(n_pieces)]

        def in_range(g):
            return 0 <= g < n_groups

        for step in range(n_groups + 4):
            if in_range(step - 1):
                reciprocal(step - 1)
            if in_range(step - 3):
                quantise(step - 3)
            if in_range(step - 4):
                project(step - 4, 1)
            if in_range(step - 3):
                project(step - 3, 0)
            for piece in range(n_pieces):
                if regroup_step[piece] == step - 1:
                    quantise_weights(piece)
                    spread_bias(piece)
            if in_range(step - 2):
                scale_and_shift(step - 2)
            if in_range(step):
                statistics(step)
            if in_range(step - 1):
                normalise_and_transpose(step - 1)
            if in_range(step - 2):
                regroup(step - 2)
            if in_range(step - 4):
                finish_on_gpsimd(step - 4)
            for piece in range(n_pieces):
                if regroup_step[piece] == step:
                    if piece < PIECES:
                        regroup_weights(piece, "vector")
                    else:
                        regroup_weights(piece, "scalar" if piece % 2 == 1 else "gpsimd")
